import numpy as np
import ml_dtypes


def mxq(x, axis, fmt="e4m3"):
    dtype, down = {"e4m3": (ml_dtypes.float8_e4m3fn, 7), "e5m2": (ml_dtypes.float8_e5m2, 14)}[fmt]
    v = np.moveaxis(np.asarray(x, np.float32).astype(ml_dtypes.bfloat16).astype(np.float64), axis, -1)
    blocks = v.reshape(v.shape[:-1] + (-1, 32))
    amax = np.abs(blocks).max(-1, keepdims=True)
    byte = np.maximum(np.where(amax > 0, np.frexp(amax)[1] - 1 + 127, 0) - down, 1)
    scale = np.exp2(byte - 127.0)
    codes = (blocks / scale).astype(np.float32).astype(dtype).astype(np.float64)
    return np.moveaxis((codes * scale).reshape(v.shape), -1, axis)


WIDE = False


def mx_kscale(k):
    if not WIDE:
        return np.ones(k)
    levels = np.array([10, -10, 5, -5, 0])
    a = np.random.permutation(np.resize(levels, k // 512 * 4)).reshape(k // 512, 4)
    idx = np.arange(k)
    return np.exp2(a[idx // 512, idx % 128 // 32])


BF16 = ml_dtypes.bfloat16


def bf(x):
    return np.asarray(x, np.float32).astype(BF16)


def f64(x):
    return np.asarray(x).astype(np.float64)


B, N, F, K = 1, 512, 512, 512
BN_EPS = 1e-5
NORM_EPS = 1e-12


def setup_inputs():
    s, t = mx_kscale(N), mx_kscale(F)
    deg = np.random.uniform(0.5, 1.5, size=(B, N, 1))
    return {"x": bf(np.random.standard_normal((B, N, F)) * 0.5 / s[:, None] * t),
            "adj": bf(np.random.uniform(size=(B, N, N)) * deg * 4.0 / np.sqrt(N) * s),
            "W": bf(np.random.standard_normal((F, K)) / np.sqrt(F) / t[:, None]),
            "b": bf(np.random.standard_normal(K) * 0.2)}


def reference(x, adj, W, b):
    agg = mxq(f64(adj), 2, "e4m3") @ mxq(f64(x), 1, "e4m3")
    h = (mxq(agg, 2, "e4m3") @ mxq(f64(W), 0, "e4m3")) + f64(b)
    nrm = np.sqrt(np.sum(h * h, axis=2, keepdims=True))
    h = h / np.maximum(nrm, NORM_EPS)
    h = np.maximum(h, 0.0)
    mean = np.mean(h, axis=(0, 2), keepdims=True)
    var = np.var(h, axis=(0, 2), keepdims=True)
    return (h - mean) / np.sqrt(var + BN_EPS)

@@ -1,0 +1,169 @@
+from contextlib import ExitStack
+
+import concourse.mybir as mybir
+from concourse.masks import make_identity
+
+F32 = mybir.dt.float32
+BF16 = mybir.dt.bfloat16
+U32 = mybir.dt.uint32
+U8 = mybir.dt.uint8
+FP8X4 = mybir.dt.float8_e4m3fn_x4
+ALU = mybir.AluOpType
+ACT = mybir.ActivationFunctionType
+
+P = 128
+PACK = 4
+SIZE = 512
+TILES = SIZE // P
+NORM_EPS = 1e-12
+BN_EPS = 1e-5
+
+FLOPS = 2 * SIZE * SIZE * SIZE * 2
+
+
+def regroup(copy, grouped, rows, first, width):
+    cols = slice(first, first + width)
+    copy(
+        out=grouped[:].rearrange("p (c t) -> p c t", t=PACK)[:, cols, :].rearrange(
+            "p (c i) t -> p c t i", i=4
+        ),
+        in_=rows[:].rearrange("p (t c) -> p t c", t=PACK)[:, :, cols].rearrange(
+            "p t (c i) -> p c t i", i=4
+        ),
+    )
+
+
+def tile_routingassignment_pa_s_kernel(tc, x, adj, W, b, out):
+    nc = tc.nc
+    with ExitStack() as ctx:
+        keep = ctx.enter_context(tc.tile_pool(name="keep", bufs=1))
+        work = ctx.enter_context(tc.tile_pool(name="work", bufs=TILES))
+        psum = ctx.enter_context(tc.psum_pool(name="psum", bufs=8))
+
+        def operand(name):
+            grouped = keep.tile([P, SIZE * PACK], BF16, name=name + "_grouped", align_bytes=64)
+            codes = keep.tile([P, SIZE], U32, name=name + "_codes", align_bytes=64)
+            scales = keep.tile([P, SIZE], U8, name=name + "_scales", align_bytes=64)
+            return grouped, codes, scales
+
+        def quantise(op, first, width):
+            grouped, codes, scales = op
+            nc.vector.quantize_mx(
+                out=codes[:, first : first + width].bitcast(FP8X4),
+                scales=scales[:, first : first + width],
+                in_=grouped[:, first * PACK : (first + width) * PACK],
+            )
+
+        def multiply(acc, stationary, s_cols, moving, m_cols):
+            nc.tensor.matmul_mx(
+                out=acc,
+                lhsT=stationary[1][:, s_cols].bitcast(FP8X4),
+                lhsT_scale=stationary[2][:, s_cols],
+                rhs=moving[1][:, m_cols].bitcast(FP8X4),
+                rhs_scale=moving[2][:, m_cols],
+                start=True,
+                stop=True,
+            )
+
+        adj_rows = keep.tile([P, TILES * SIZE], BF16)
+        adj_view = adj[0].rearrange("(p i) m -> p (i m)", i=TILES)
+        half = TILES * SIZE // 2
+        nc.sync.dma_start(out=adj_rows[:, :half], in_=adj_view[:, :half])
+        nc.sync.dma_start(out=adj_rows[:, half:], in_=adj_view[:, half:])
+        x_rows = keep.tile([P, PACK * SIZE], BF16)
+        nc.sync.dma_start(
+            out=x_rows[:].rearrange("p (u r) -> p u r", u=2),
+            in_=x[0].rearrange("(u p e) f -> p u (e f)", u=2, e=2),
+        )
+        w_rows = keep.tile([P, PACK * SIZE], BF16)
+        nc.sync.dma_start(
+            out=w_rows[:].rearrange("p (t k) -> p t k", t=PACK),
+            in_=W.rearrange("(t p) k -> p t k", p=P),
+        )
+
+        one = keep.tile([P, 1], F32)
+        nc.vector.memset(one[:], 1.0)
+        nc.scalar.activation(out=one[:], in_=one[:], func=ACT.Sqrt)
+        ident = keep.tile([P, P], F32)
+        make_identity(nc, ident[:])
+
+        b_rows = keep.tile([P, SIZE], BF16)
+        nc.vector.memset(b_rows[:], 0.0)
+        nc.scalar.dma_start(out=b_rows[0:1, :], in_=b.unsqueeze(0))
+        ones = keep.tile([P, P], BF16)
+        nc.vector.memset(ones[:], 1.0)
+        b_bank = psum.tile([P, SIZE], F32, tag="bank")
+        nc.tensor.matmul(out=b_bank[:], lhsT=ones[:], rhs=b_rows[:], start=True, stop=True)
+        b_all = keep.tile([P, SIZE], F32)
+        nc.scalar.copy(out=b_all[:], in_=b_bank[:])
+
+        adj_op = operand("adj")
+        adj_words = adj_rows[:].bitcast(F32)
+        adj_pairs = adj_op[0][:].bitcast(F32).rearrange("p (n u) -> p n u", u=2)
+        for j in range(2):
+            adjT = psum.tile([P, 2, 2, P], F32, tag="bank")
+            for i in range(2):
+                for u in range(2):
+                    first = ((2 * j + i) * 2 + u) * P
+                    nc.tensor.transpose(adjT[:, i, u, :], adj_words[:, first : first + P], ident[:])
+            copy = nc.vector.tensor_copy if j == 0 else nc.scalar.copy
+            copy(
+                out=adj_pairs[:, 2 * j * P : (2 * j + 2) * P, :].rearrange("p (i n) u -> p i n u", i=2),
+                in_=adjT[:].rearrange("p i u n -> p i n u"),
+            )
+
+        x_op = operand("x")
+        regroup(nc.vector.tensor_copy, x_op[0], x_rows, 0, 3 * P)
+        regroup(nc.scalar.copy, x_op[0], x_rows, 3 * P, P)
+        quantise(adj_op, 0, 2 * P)
+        quantise(adj_op, 2 * P, 2 * P)
+        quantise(x_op, 0, SIZE)
+
+        w_op = operand("w")
+        regroup(nc.vector.tensor_copy, w_op[0], w_rows, 0, 2 * P)
+        regroup(nc.scalar.copy, w_op[0], w_rows, 2 * P, 2 * P)
+        quantise(w_op, 0, SIZE)
+
+        agg_op = operand("agg")
+        agg_words = agg_op[0][:].rearrange("p (n t) -> p n t", t=PACK)
+        for i in range(TILES):
+            nodes = slice(i * P, (i + 1) * P)
+            aggT = psum.tile([P, PACK, P], F32, tag="bank")
+            for t in range(PACK):
+                multiply(aggT[:, t, :], x_op, slice(t * P, (t + 1) * P), adj_op, nodes)
+            copy = nc.scalar.copy if i % 2 == 0 else nc.vector.tensor_copy
+            copy(out=agg_words[:, nodes, :], in_=aggT[:].rearrange("p t n -> p n t"))
+            quantise(agg_op, i * P, P)
+
+        out_view = out[0].rearrange("(p i) k -> p i k", i=TILES)
+        for i in range(TILES):
+            h_bank = psum.tile([P, SIZE], F32, tag="bank")
+            multiply(h_bank[:], agg_op, slice(i * P, (i + 1) * P), w_op, slice(0, SIZE))
+            h = work.tile([P, SIZE], F32)
+            nc.vector.tensor_tensor(out=h[:], in0=h_bank[:], in1=b_all[:], op=ALU.add)
+
+            squares = work.tile([P, SIZE], F32)
+            sumsq = work.tile([P, 1], F32)
+            nc.scalar.activation(out=squares[:], in_=h[:], func=ACT.Square, accum_out=sumsq[:])
+            g = work.tile([P, SIZE], F32)
+            nc.scalar.activation(out=g[:], in_=h[:], func=ACT.Relu)
+            stats = work.tile([P, 6], F32)
+            nc.vector.bn_stats(out=stats[:], in_=g[:])
+            mean_var = work.tile([P, 2], F32)
+            nc.vector.bn_aggr(out=mean_var[:], in_=stats[:])
+
+            eps_term = work.tile([P, 1], F32)
+            nc.vector.tensor_scalar(
+                out=eps_term[:], in0=sumsq[:], scalar1=NORM_EPS * NORM_EPS, scalar2=BN_EPS,
+                op0=ALU.max, op1=ALU.mult,
+            )
+            spread = work.tile([P, 1], F32)
+            nc.scalar.activation(out=spread[:], in_=eps_term[:], func=ACT.Sqrt, bias=mean_var[:, 1:2])
+            inv_spread = work.tile([P, 1], F32)
+            nc.vector.reciprocal(out=inv_spread[:], in_=spread[:])
+            result = work.tile([P, SIZE], F32)
+            nc.vector.tensor_scalar(
+                out=result[:], in0=g[:], scalar1=mean_var[:, 0:1], scalar2=inv_spread[:],
+                op0=ALU.subtract, op1=ALU.mult,
+            )
+            nc.sync.dma_start(out=out_view[:, i, :], in_=result[:])

@@ -39,6 +39,7 @@ def tile_routingassignment_pa_s_kernel(tc, x, adj, W, b, out):
         keep = ctx.enter_context(tc.tile_pool(name="keep", bufs=1))
         work = ctx.enter_context(tc.tile_pool(name="work", bufs=TILES))
         psum = ctx.enter_context(tc.psum_pool(name="psum", bufs=8))
+        ctx.enter_context(tc.manual_schedule())
 
         def operand(name):
             grouped = keep.tile([P, SIZE * PACK], BF16, name=name + "_grouped", align_bytes=64)
@@ -54,116 +55,129 @@ def tile_routingassignment_pa_s_kernel(tc, x, adj, W, b, out):
                 in_=grouped[:, first * PACK : (first + width) * PACK],
             )
 
-        def multiply(acc, stationary, s_cols, moving, m_cols):
+        def multiply(acc, stationary, s_first, moving, m_first, m_width):
             nc.tensor.matmul_mx(
                 out=acc,
-                lhsT=stationary[1][:, s_cols].bitcast(FP8X4),
-                lhsT_scale=stationary[2][:, s_cols],
-                rhs=moving[1][:, m_cols].bitcast(FP8X4),
-                rhs_scale=moving[2][:, m_cols],
+                lhsT=stationary[1][:, s_first : s_first + P].bitcast(FP8X4),
+                lhsT_scale=stationary[2][:, s_first : s_first + P],
+                rhs=moving[1][:, m_first : m_first + m_width].bitcast(FP8X4),
+                rhs_scale=moving[2][:, m_first : m_first + m_width],
                 start=True,
                 stop=True,
             )
 
-        adj_rows = keep.tile([P, TILES * SIZE], BF16)
-        adj_view = adj[0].rearrange("(p i) m -> p (i m)", i=TILES)
-        half = TILES * SIZE // 2
-        nc.sync.dma_start(out=adj_rows[:, :half], in_=adj_view[:, :half])
-        nc.sync.dma_start(out=adj_rows[:, half:], in_=adj_view[:, half:])
         x_rows = keep.tile([P, PACK * SIZE], BF16)
         nc.sync.dma_start(
             out=x_rows[:].rearrange("p (u r) -> p u r", u=2),
             in_=x[0].rearrange("(u p e) f -> p u (e f)", u=2, e=2),
         )
+        adj_rows = keep.tile([P, TILES * SIZE], BF16)
+        adj_view = adj[0].rearrange("(p i) m -> p (i m)", i=TILES)
+        for i in range(TILES):
+            nc.sync.dma_start(
+                out=adj_rows[:, i * SIZE : (i + 1) * SIZE], in_=adj_view[:, i * SIZE : (i + 1) * SIZE]
+            )
         w_rows = keep.tile([P, PACK * SIZE], BF16)
         nc.sync.dma_start(
             out=w_rows[:].rearrange("p (t k) -> p t k", t=PACK),
             in_=W.rearrange("(t p) k -> p t k", p=P),
         )
 
-        one = keep.tile([P, 1], F32)
-        nc.vector.memset(one[:], 1.0)
-        nc.scalar.activation(out=one[:], in_=one[:], func=ACT.Sqrt)
-        ident = keep.tile([P, P], F32)
-        make_identity(nc, ident[:])
-
         b_rows = keep.tile([P, SIZE], BF16)
         nc.vector.memset(b_rows[:], 0.0)
         nc.scalar.dma_start(out=b_rows[0:1, :], in_=b.unsqueeze(0))
         ones = keep.tile([P, P], BF16)
         nc.vector.memset(ones[:], 1.0)
+        one = keep.tile([P, 1], F32)
+        nc.vector.memset(one[:], 1.0)
+        nc.scalar.activation(out=one[:], in_=one[:], func=ACT.Abs_reciprocal_sqrt)
+        ident = keep.tile([P, P], F32)
+        make_identity(nc, ident[:])
+
+        x_op = operand("x")
+        regroup(nc.vector.tensor_copy, x_op[0], x_rows, 0, 3 * P)
+        regroup(nc.scalar.copy, x_op[0], x_rows, 3 * P, P)
+        quantise(x_op, 0, SIZE)
+
+        adj_op = operand("adj")
+        adj_words = adj_rows[:].bitcast(F32)
+        adj_pairs = adj_op[0][:].bitcast(F32).rearrange("p (n u) -> p n u", u=2)
+        for i in range(TILES):
+            adjT = psum.tile([P, 2, P], F32, tag="bank")
+            for u in range(2):
+                first = (2 * i + u) * P
+                nc.tensor.transpose(adjT[:, u, :], adj_words[:, first : first + P], ident[:])
+            nc.scalar.copy(
+                out=adj_pairs[:, i * P : (i + 1) * P, :], in_=adjT[:].rearrange("p u n -> p n u")
+            )
+            quantise(adj_op, i * P, P)
+
         b_bank = psum.tile([P, SIZE], F32, tag="bank")
         nc.tensor.matmul(out=b_bank[:], lhsT=ones[:], rhs=b_rows[:], start=True, stop=True)
         b_all = keep.tile([P, SIZE], F32)
         nc.scalar.copy(out=b_all[:], in_=b_bank[:])
 
-        adj_op = operand("adj")
-        adj_words = adj_rows[:].bitcast(F32)
-        adj_pairs = adj_op[0][:].bitcast(F32).rearrange("p (n u) -> p n u", u=2)
-        for j in range(2):
-            adjT = psum.tile([P, 2, 2, P], F32, tag="bank")
-            for i in range(2):
-                for u in range(2):
-                    first = ((2 * j + i) * 2 + u) * P
-                    nc.tensor.transpose(adjT[:, i, u, :], adj_words[:, first : first + P], ident[:])
-            copy = nc.vector.tensor_copy if j == 0 else nc.scalar.copy
-            copy(
-                out=adj_pairs[:, 2 * j * P : (2 * j + 2) * P, :].rearrange("p (i n) u -> p i n u", i=2),
-                in_=adjT[:].rearrange("p i u n -> p i n u"),
-            )
-
-        x_op = operand("x")
-        regroup(nc.vector.tensor_copy, x_op[0], x_rows, 0, 3 * P)
-        regroup(nc.scalar.copy, x_op[0], x_rows, 3 * P, P)
-        quantise(adj_op, 0, 2 * P)
-        quantise(adj_op, 2 * P, 2 * P)
-        quantise(x_op, 0, SIZE)
-
         w_op = operand("w")
-        regroup(nc.vector.tensor_copy, w_op[0], w_rows, 0, 2 * P)
-        regroup(nc.scalar.copy, w_op[0], w_rows, 2 * P, 2 * P)
+        regroup(nc.vector.tensor_copy, w_op[0], w_rows, 0, SIZE)
         quantise(w_op, 0, SIZE)
 
         agg_op = operand("agg")
         agg_words = agg_op[0][:].rearrange("p (n t) -> p n t", t=PACK)
         for i in range(TILES):
-            nodes = slice(i * P, (i + 1) * P)
             aggT = psum.tile([P, PACK, P], F32, tag="bank")
             for t in range(PACK):
-                multiply(aggT[:, t, :], x_op, slice(t * P, (t + 1) * P), adj_op, nodes)
-            copy = nc.scalar.copy if i % 2 == 0 else nc.vector.tensor_copy
-            copy(out=agg_words[:, nodes, :], in_=aggT[:].rearrange("p t n -> p n t"))
+                multiply(aggT[:, t, :], x_op, t * P, adj_op, i * P, P)
+            nc.scalar.copy(
+                out=agg_words[:, i * P : (i + 1) * P, :], in_=aggT[:].rearrange("p t n -> p n t")
+            )
             quantise(agg_op, i * P, P)
 
         out_view = out[0].rearrange("(p i) k -> p i k", i=TILES)
-        for i in range(TILES):
+        h, g, sumsq, mean_var, inv_spread = {}, {}, {}, {}, {}
+
+        def product_and_relu(i):
             h_bank = psum.tile([P, SIZE], F32, tag="bank")
-            multiply(h_bank[:], agg_op, slice(i * P, (i + 1) * P), w_op, slice(0, SIZE))
-            h = work.tile([P, SIZE], F32)
-            nc.vector.tensor_tensor(out=h[:], in0=h_bank[:], in1=b_all[:], op=ALU.add)
+            multiply(h_bank[:], agg_op, i * P, w_op, 0, SIZE)
+            h[i] = work.tile([P, SIZE], F32, name="h")
+            nc.vector.tensor_tensor(out=h[i][:], in0=h_bank[:], in1=b_all[:], op=ALU.add)
+            g[i] = work.tile([P, SIZE], F32, name="g")
+            nc.scalar.activation(out=g[i][:], in_=h[i][:], func=ACT.Relu)
 
+        def sum_of_squares(i):
             squares = work.tile([P, SIZE], F32)
-            sumsq = work.tile([P, 1], F32)
-            nc.scalar.activation(out=squares[:], in_=h[:], func=ACT.Square, accum_out=sumsq[:])
-            g = work.tile([P, SIZE], F32)
-            nc.scalar.activation(out=g[:], in_=h[:], func=ACT.Relu)
-            stats = work.tile([P, 6], F32)
-            nc.vector.bn_stats(out=stats[:], in_=g[:])
-            mean_var = work.tile([P, 2], F32)
-            nc.vector.bn_aggr(out=mean_var[:], in_=stats[:])
+            sumsq[i] = work.tile([P, 1], F32, name="sumsq")
+            nc.scalar.activation(out=squares[:], in_=h[i][:], func=ACT.Square, accum_out=sumsq[i][:])
 
+        def statistics(i):
+            stats = work.tile([P, 6], F32)
+            nc.vector.bn_stats(out=stats[:], in_=g[i][:])
+            mean_var[i] = work.tile([P, 2], F32, name="mean_var")
+            nc.vector.bn_aggr(out=mean_var[i][:], in_=stats[:])
             eps_term = work.tile([P, 1], F32)
             nc.vector.tensor_scalar(
-                out=eps_term[:], in0=sumsq[:], scalar1=NORM_EPS * NORM_EPS, scalar2=BN_EPS,
+                out=eps_term[:], in0=sumsq[i][:], scalar1=NORM_EPS * NORM_EPS, scalar2=BN_EPS,
                 op0=ALU.max, op1=ALU.mult,
             )
-            spread = work.tile([P, 1], F32)
-            nc.scalar.activation(out=spread[:], in_=eps_term[:], func=ACT.Sqrt, bias=mean_var[:, 1:2])
-            inv_spread = work.tile([P, 1], F32)
-            nc.vector.reciprocal(out=inv_spread[:], in_=spread[:])
+            inv_spread[i] = work.tile([P, 1], F32, name="inv_spread")
+            nc.scalar.activation(
+                out=inv_spread[i][:], in_=eps_term[:], func=ACT.Abs_reciprocal_sqrt,
+                bias=mean_var[i][:, 1:2],
+            )
+
+        def normalise_and_store(i):
             result = work.tile([P, SIZE], F32)
             nc.vector.tensor_scalar(
-                out=result[:], in0=g[:], scalar1=mean_var[:, 0:1], scalar2=inv_spread[:],
+                out=result[:], in0=g[i][:], scalar1=mean_var[i][:, 0:1], scalar2=inv_spread[i][:],
                 op0=ALU.subtract, op1=ALU.mult,
             )
             nc.sync.dma_start(out=out_view[:, i, :], in_=result[:])
+
+        for step in range(TILES + 2):
+            if step < TILES:
+                product_and_relu(step)
+            if 1 <= step <= TILES:
+                statistics(step - 1)
+            if step < TILES:
+                sum_of_squares(step)
+            if step >= 2:
+                normalise_and_store(step - 2)

@@ -39,7 +39,6 @@ def tile_routingassignment_pa_s_kernel(tc, x, adj, W, b, out):
         keep = ctx.enter_context(tc.tile_pool(name="keep", bufs=1))
         work = ctx.enter_context(tc.tile_pool(name="work", bufs=TILES))
         psum = ctx.enter_context(tc.psum_pool(name="psum", bufs=8))
-        ctx.enter_context(tc.manual_schedule())
 
         def operand(name):
             grouped = keep.tile([P, SIZE * PACK], BF16, name=name + "_grouped", align_bytes=64)

@@ -39,6 +39,7 @@ def tile_routingassignment_pa_s_kernel(tc, x, adj, W, b, out):
         keep = ctx.enter_context(tc.tile_pool(name="keep", bufs=1))
         work = ctx.enter_context(tc.tile_pool(name="work", bufs=TILES))
         psum = ctx.enter_context(tc.psum_pool(name="psum", bufs=8))
+        ctx.enter_context(tc.manual_schedule())
 
         def operand(name):
             grouped = keep.tile([P, SIZE * PACK], BF16, name=name + "_grouped", align_bytes=64)
@@ -94,9 +95,11 @@ def tile_routingassignment_pa_s_kernel(tc, x, adj, W, b, out):
         make_identity(nc, ident[:])
 
         x_op = operand("x")
-        regroup(nc.vector.tensor_copy, x_op[0], x_rows, 0, 3 * P)
+        regroup(nc.vector.tensor_copy, x_op[0], x_rows, 0, 2 * P)
+        regroup(nc.vector.tensor_copy, x_op[0], x_rows, 2 * P, P)
         regroup(nc.scalar.copy, x_op[0], x_rows, 3 * P, P)
-        quantise(x_op, 0, SIZE)
+        quantise(x_op, 0, 2 * P)
+        quantise(x_op, 2 * P, 2 * P)
 
         adj_op = operand("adj")
         adj_words = adj_rows[:].bitcast(F32)
@@ -117,8 +120,10 @@ def tile_routingassignment_pa_s_kernel(tc, x, adj, W, b, out):
         nc.scalar.copy(out=b_all[:], in_=b_bank[:])
 
         w_op = operand("w")
-        regroup(nc.vector.tensor_copy, w_op[0], w_rows, 0, SIZE)
-        quantise(w_op, 0, SIZE)
+        regroup(nc.vector.tensor_copy, w_op[0], w_rows, 0, 2 * P)
+        regroup(nc.vector.tensor_copy, w_op[0], w_rows, 2 * P, 2 * P)
+        quantise(w_op, 0, 2 * P)
+        quantise(w_op, 2 * P, 2 * P)
 
         agg_op = operand("agg")
         agg_words = agg_op[0][:].rearrange("p (n t) -> p n t", t=PACK)
@@ -132,7 +137,7 @@ def tile_routingassignment_pa_s_kernel(tc, x, adj, W, b, out):
             quantise(agg_op, i * P, P)
 
         out_view = out[0].rearrange("(p i) k -> p i k", i=TILES)
-        h, g, sumsq, mean_var, inv_spread = {}, {}, {}, {}, {}
+        h, g, sumsq, stats, mean_var, inv_spread = {}, {}, {}, {}, {}, {}
 
         def product_and_relu(i):
             h_bank = psum.tile([P, SIZE], F32, tag="bank")
@@ -147,11 +152,13 @@ def tile_routingassignment_pa_s_kernel(tc, x, adj, W, b, out):
             sumsq[i] = work.tile([P, 1], F32, name="sumsq")
             nc.scalar.activation(out=squares[:], in_=h[i][:], func=ACT.Square, accum_out=sumsq[i][:])
 
-        def statistics(i):
-            stats = work.tile([P, 6], F32)
-            nc.vector.bn_stats(out=stats[:], in_=g[i][:])
+        def moments(i):
+            stats[i] = work.tile([P, 6], F32, name="stats")
+            nc.vector.bn_stats(out=stats[i][:], in_=g[i][:])
+
+        def spread(i):
             mean_var[i] = work.tile([P, 2], F32, name="mean_var")
-            nc.vector.bn_aggr(out=mean_var[i][:], in_=stats[:])
+            nc.vector.bn_aggr(out=mean_var[i][:], in_=stats[i][:])
             eps_term = work.tile([P, 1], F32)
             nc.vector.tensor_scalar(
                 out=eps_term[:], in0=sumsq[i][:], scalar1=NORM_EPS * NORM_EPS, scalar2=BN_EPS,
@@ -175,8 +182,10 @@ def tile_routingassignment_pa_s_kernel(tc, x, adj, W, b, out):
             if step < TILES:
                 product_and_relu(step)
             if 1 <= step <= TILES:
-                statistics(step - 1)
-            if step < TILES:
-                sum_of_squares(step)
+                moments(step - 1)
             if step >= 2:
                 normalise_and_store(step - 2)
+            if 1 <= step <= TILES:
+                spread(step - 1)
+            if step < TILES:
+                sum_of_squares(step)

@@ -82,12 +82,9 @@ def tile_routingassignment_pa_s_kernel(tc, x, adj, W, b, out):
             out=w_rows[:].rearrange("p (t k) -> p t k", t=PACK),
             in_=W.rearrange("(t p) k -> p t k", p=P),
         )
+        b_all = keep.tile([P, SIZE], BF16)
+        nc.sync.dma_start(out=b_all[:], in_=b.partition_broadcast(P))
 
-        b_rows = keep.tile([P, SIZE], BF16)
-        nc.vector.memset(b_rows[:], 0.0)
-        nc.scalar.dma_start(out=b_rows[0:1, :], in_=b.unsqueeze(0))
-        ones = keep.tile([P, P], BF16)
-        nc.vector.memset(ones[:], 1.0)
         one = keep.tile([P, 1], F32)
         nc.vector.memset(one[:], 1.0)
         nc.scalar.activation(out=one[:], in_=one[:], func=ACT.Abs_reciprocal_sqrt)
@@ -112,12 +109,8 @@ def tile_routingassignment_pa_s_kernel(tc, x, adj, W, b, out):
             nc.scalar.copy(
                 out=adj_pairs[:, i * P : (i + 1) * P, :], in_=adjT[:].rearrange("p u n -> p n u")
             )
-            quantise(adj_op, i * P, P)
-
-        b_bank = psum.tile([P, SIZE], F32, tag="bank")
-        nc.tensor.matmul(out=b_bank[:], lhsT=ones[:], rhs=b_rows[:], start=True, stop=True)
-        b_all = keep.tile([P, SIZE], F32)
-        nc.scalar.copy(out=b_all[:], in_=b_bank[:])
+        quantise(adj_op, 0, 2 * P)
+        quantise(adj_op, 2 * P, 2 * P)
 
         w_op = operand("w")
         regroup(nc.vector.tensor_copy, w_op[0], w_rows, 0, 2 * P)
@@ -137,13 +130,18 @@ def tile_routingassignment_pa_s_kernel(tc, x, adj, W, b, out):
             quantise(agg_op, i * P, P)
 
         out_view = out[0].rearrange("(p i) k -> p i k", i=TILES)
-        h, g, sumsq, stats, mean_var, inv_spread = {}, {}, {}, {}, {}, {}
+        h_bank = {}
+        h, g, sumsq, stats, eps_term, mean_var, inv_spread = {}, {}, {}, {}, {}, {}, {}
 
-        def product_and_relu(i):
-            h_bank = psum.tile([P, SIZE], F32, tag="bank")
-            multiply(h_bank[:], agg_op, i * P, w_op, 0, SIZE)
+        def product(i):
+            h_bank[i] = psum.tile([P, SIZE], F32, tag="bank", name="h_bank")
+            multiply(h_bank[i][:], agg_op, i * P, w_op, 0, SIZE)
+
+        def add_bias(i):
             h[i] = work.tile([P, SIZE], F32, name="h")
-            nc.vector.tensor_tensor(out=h[i][:], in0=h_bank[:], in1=b_all[:], op=ALU.add)
+            nc.vector.tensor_tensor(out=h[i][:], in0=h_bank[i][:], in1=b_all[:], op=ALU.add)
+
+        def relu(i):
             g[i] = work.tile([P, SIZE], F32, name="g")
             nc.scalar.activation(out=g[i][:], in_=h[i][:], func=ACT.Relu)
 
@@ -156,36 +154,66 @@ def tile_routingassignment_pa_s_kernel(tc, x, adj, W, b, out):
             stats[i] = work.tile([P, 6], F32, name="stats")
             nc.vector.bn_stats(out=stats[i][:], in_=g[i][:])
 
-        def spread(i):
+        def aggregate_moments(i):
             mean_var[i] = work.tile([P, 2], F32, name="mean_var")
             nc.vector.bn_aggr(out=mean_var[i][:], in_=stats[i][:])
-            eps_term = work.tile([P, 1], F32)
+
+        def epsilon_term(i):
+            eps_term[i] = work.tile([P, 1], F32, name="eps_term")
             nc.vector.tensor_scalar(
-                out=eps_term[:], in0=sumsq[i][:], scalar1=NORM_EPS * NORM_EPS, scalar2=BN_EPS,
+                out=eps_term[i][:], in0=sumsq[i][:], scalar1=NORM_EPS * NORM_EPS, scalar2=BN_EPS,
                 op0=ALU.max, op1=ALU.mult,
             )
+
+        def inverse_root(i):
             inv_spread[i] = work.tile([P, 1], F32, name="inv_spread")
             nc.scalar.activation(
-                out=inv_spread[i][:], in_=eps_term[:], func=ACT.Abs_reciprocal_sqrt,
+                out=inv_spread[i][:], in_=eps_term[i][:], func=ACT.Abs_reciprocal_sqrt,
                 bias=mean_var[i][:, 1:2],
             )
 
-        def normalise_and_store(i):
-            result = work.tile([P, SIZE], F32)
+        def store(i, result):
+            nc.sync.dma_start(out=out_view[:, i, :], in_=result[:])
+
+        def normalise(i):
+            result = work.tile([P, SIZE], F32, name="result")
             nc.vector.tensor_scalar(
                 out=result[:], in0=g[i][:], scalar1=mean_var[i][:, 0:1], scalar2=inv_spread[i][:],
                 op0=ALU.subtract, op1=ALU.mult,
             )
-            nc.sync.dma_start(out=out_view[:, i, :], in_=result[:])
+            store(i, result)
 
-        for step in range(TILES + 2):
-            if step < TILES:
-                product_and_relu(step)
-            if 1 <= step <= TILES:
-                moments(step - 1)
-            if step >= 2:
-                normalise_and_store(step - 2)
-            if 1 <= step <= TILES:
-                spread(step - 1)
-            if step < TILES:
-                sum_of_squares(step)
+        for i in range(TILES):
+            product(i)
+        add_bias(0)
+        add_bias(1)
+        add_bias(2)
+        relu(0)
+        sum_of_squares(0)
+        relu(1)
+        moments(0)
+        epsilon_term(0)
+        aggregate_moments(0)
+        sum_of_squares(1)
+        inverse_root(0)
+        add_bias(3)
+        moments(1)
+        relu(2)
+        normalise(0)
+        epsilon_term(1)
+        aggregate_moments(1)
+        sum_of_squares(2)
+        inverse_root(1)
+        moments(2)
+        normalise(1)
+        relu(3)
+        epsilon_term(2)
+        aggregate_moments(2)
+        sum_of_squares(3)
+        inverse_root(2)
+        moments(3)
+        epsilon_term(3)
+        aggregate_moments(3)
+        inverse_root(3)
+        normalise(2)
+        normalise(3)

@@ -82,9 +82,17 @@ def tile_routingassignment_pa_s_kernel(tc, x, adj, W, b, out):
             out=w_rows[:].rearrange("p (t k) -> p t k", t=PACK),
             in_=W.rearrange("(t p) k -> p t k", p=P),
         )
-        b_all = keep.tile([P, SIZE], BF16)
-        nc.sync.dma_start(out=b_all[:], in_=b.partition_broadcast(P))
 
+        b_rows = keep.tile([P, SIZE], BF16)
+        nc.vector.memset(b_rows[:].bitcast(U32), 0)
+        nc.scalar.dma_start(out=b_rows[0:1, :], in_=b.unsqueeze(0))
+        ones = keep.tile([P, P], BF16)
+        nc.vector.memset(ones[:], 1.0)
+        blank = keep.tile([P, SIZE], BF16)
+        nc.vector.memset(blank[:].bitcast(U32), 0)
+        warm = psum.tile([P, SIZE], F32, tag="bank")
+        for turn in range(2):
+            nc.tensor.matmul(out=warm[:], lhsT=ones[:], rhs=blank[:], start=True, stop=True)
         one = keep.tile([P, 1], F32)
         nc.vector.memset(one[:], 1.0)
         nc.scalar.activation(out=one[:], in_=one[:], func=ACT.Abs_reciprocal_sqrt)
@@ -109,8 +117,13 @@ def tile_routingassignment_pa_s_kernel(tc, x, adj, W, b, out):
             nc.scalar.copy(
                 out=adj_pairs[:, i * P : (i + 1) * P, :], in_=adjT[:].rearrange("p u n -> p n u")
             )
-        quantise(adj_op, 0, 2 * P)
-        quantise(adj_op, 2 * P, 2 * P)
+        b_bank = psum.tile([P, SIZE], F32, tag="bank")
+        nc.tensor.matmul(out=b_bank[:], lhsT=ones[:], rhs=b_rows[:], start=True, stop=True)
+        b_all = keep.tile([P, SIZE], F32)
+        nc.scalar.copy(out=b_all[:], in_=b_bank[:])
+
+        for i in range(TILES):
+            quantise(adj_op, i * P, P)
 
         w_op = operand("w")
         regroup(nc.vector.tensor_copy, w_op[0], w_rows, 0, 2 * P)

@@ -122,8 +122,9 @@ def tile_routingassignment_pa_s_kernel(tc, x, adj, W, b, out):
         b_all = keep.tile([P, SIZE], F32)
         nc.scalar.copy(out=b_all[:], in_=b_bank[:])
 
-        for i in range(TILES):
-            quantise(adj_op, i * P, P)
+        quantise(adj_op, 0, P)
+        quantise(adj_op, P, P)
+        quantise(adj_op, 2 * P, 2 * P)
 
         w_op = operand("w")
         regroup(nc.vector.tensor_copy, w_op[0], w_rows, 0, 2 * P)
@@ -140,7 +141,9 @@ def tile_routingassignment_pa_s_kernel(tc, x, adj, W, b, out):
             nc.scalar.copy(
                 out=agg_words[:, i * P : (i + 1) * P, :], in_=aggT[:].rearrange("p t n -> p n t")
             )
-            quantise(agg_op, i * P, P)
+            if i != 1:
+                first = P if i == 2 else i * P
+                quantise(agg_op, first, (i + 1) * P - first)
 
         out_view = out[0].rearrange("(p i) k -> p i k", i=TILES)
         h_bank = {}
@@ -205,11 +208,11 @@ def tile_routingassignment_pa_s_kernel(tc, x, adj, W, b, out):
         sum_of_squares(0)
         relu(1)
         moments(0)
+        add_bias(3)
         epsilon_term(0)
         aggregate_moments(0)
         sum_of_squares(1)
         inverse_root(0)
-        add_bias(3)
         moments(1)
         relu(2)
         normalise(0)
@@ -218,8 +221,8 @@ def tile_routingassignment_pa_s_kernel(tc, x, adj, W, b, out):
         sum_of_squares(2)
         inverse_root(1)
         moments(2)
-        normalise(1)
         relu(3)
+        normalise(1)
         epsilon_term(2)
         aggregate_moments(2)
         sum_of_squares(3)

@@ -88,16 +88,14 @@ def tile_routingassignment_pa_s_kernel(tc, x, adj, W, b, out):
         nc.scalar.dma_start(out=b_rows[0:1, :], in_=b.unsqueeze(0))
         ones = keep.tile([P, P], BF16)
         nc.vector.memset(ones[:], 1.0)
-        blank = keep.tile([P, SIZE], BF16)
-        nc.vector.memset(blank[:].bitcast(U32), 0)
-        warm = psum.tile([P, SIZE], F32, tag="bank")
-        for turn in range(2):
-            nc.tensor.matmul(out=warm[:], lhsT=ones[:], rhs=blank[:], start=True, stop=True)
         one = keep.tile([P, 1], F32)
         nc.vector.memset(one[:], 1.0)
         nc.scalar.activation(out=one[:], in_=one[:], func=ACT.Abs_reciprocal_sqrt)
         ident = keep.tile([P, P], F32)
         make_identity(nc, ident[:])
+        warm = psum.tile([P, SIZE], F32, tag="bank")
+        for turn in range(5):
+            nc.tensor.matmul(out=warm[:, 0:P], lhsT=ident[:], rhs=ident[:], start=True, stop=True)
 
         x_op = operand("x")
         regroup(nc.vector.tensor_copy, x_op[0], x_rows, 0, 2 * P)

from contextlib import ExitStack

import concourse.mybir as mybir
from concourse.masks import make_identity

F32 = mybir.dt.float32
BF16 = mybir.dt.bfloat16
U32 = mybir.dt.uint32
U8 = mybir.dt.uint8
FP8X4 = mybir.dt.float8_e4m3fn_x4
ALU = mybir.AluOpType
ACT = mybir.ActivationFunctionType

P = 128
PACK = 4
SIZE = 512
TILES = SIZE // P
NORM_EPS = 1e-12
BN_EPS = 1e-5

FLOPS = 2 * SIZE * SIZE * SIZE * 2


def regroup(copy, grouped, rows, first, width):
    cols = slice(first, first + width)
    copy(
        out=grouped[:].rearrange("p (c t) -> p c t", t=PACK)[:, cols, :].rearrange(
            "p (c i) t -> p c t i", i=4
        ),
        in_=rows[:].rearrange("p (t c) -> p t c", t=PACK)[:, :, cols].rearrange(
            "p t (c i) -> p c t i", i=4
        ),
    )


def tile_routingassignment_pa_s_kernel(tc, x, adj, W, b, out):
    nc = tc.nc
    with ExitStack() as ctx:
        keep = ctx.enter_context(tc.tile_pool(name="keep", bufs=1))
        work = ctx.enter_context(tc.tile_pool(name="work", bufs=TILES))
        psum = ctx.enter_context(tc.psum_pool(name="psum", bufs=8))
        ctx.enter_context(tc.manual_schedule())

        def operand(name):
            grouped = keep.tile([P, SIZE * PACK], BF16, name=name + "_grouped", align_bytes=64)
            codes = keep.tile([P, SIZE], U32, name=name + "_codes", align_bytes=64)
            scales = keep.tile([P, SIZE], U8, name=name + "_scales", align_bytes=64)
            return grouped, codes, scales

        def quantise(op, first, width):
            grouped, codes, scales = op
            nc.vector.quantize_mx(
                out=codes[:, first : first + width].bitcast(FP8X4),
                scales=scales[:, first : first + width],
                in_=grouped[:, first * PACK : (first + width) * PACK],
            )

        def multiply(acc, stationary, s_first, moving, m_first, m_width):
            nc.tensor.matmul_mx(
                out=acc,
                lhsT=stationary[1][:, s_first : s_first + P].bitcast(FP8X4),
                lhsT_scale=stationary[2][:, s_first : s_first + P],
                rhs=moving[1][:, m_first : m_first + m_width].bitcast(FP8X4),
                rhs_scale=moving[2][:, m_first : m_first + m_width],
                start=True,
                stop=True,
            )

        x_rows = keep.tile([P, PACK * SIZE], BF16)
        nc.sync.dma_start(
            out=x_rows[:].rearrange("p (u r) -> p u r", u=2),
            in_=x[0].rearrange("(u p e) f -> p u (e f)", u=2, e=2),
        )
        adj_rows = keep.tile([P, TILES * SIZE], BF16)
        adj_view = adj[0].rearrange("(p i) m -> p (i m)", i=TILES)
        for i in range(TILES):
            nc.sync.dma_start(
                out=adj_rows[:, i * SIZE : (i + 1) * SIZE], in_=adj_view[:, i * SIZE : (i + 1) * SIZE]
            )
        w_rows = keep.tile([P, PACK * SIZE], BF16)
        nc.sync.dma_start(
            out=w_rows[:].rearrange("p (t k) -> p t k", t=PACK),
            in_=W.rearrange("(t p) k -> p t k", p=P),
        )

        b_rows = keep.tile([P, SIZE], BF16)
        nc.vector.memset(b_rows[:].bitcast(U32), 0)
        nc.scalar.dma_start(out=b_rows[0:1, :], in_=b.unsqueeze(0))
        ones = keep.tile([P, P], BF16)
        nc.vector.memset(ones[:], 1.0)
        one = keep.tile([P, 1], F32)
        nc.vector.memset(one[:], 1.0)
        nc.scalar.activation(out=one[:], in_=one[:], func=ACT.Abs_reciprocal_sqrt)
        ident = keep.tile([P, P], F32)
        make_identity(nc, ident[:])
        warm = psum.tile([P, SIZE], F32, tag="bank")
        for turn in range(5):
            nc.tensor.matmul(out=warm[:, 0:P], lhsT=ident[:], rhs=ident[:], start=True, stop=True)

        x_op = operand("x")
        regroup(nc.vector.tensor_copy, x_op[0], x_rows, 0, 2 * P)
        regroup(nc.vector.tensor_copy, x_op[0], x_rows, 2 * P, P)
        regroup(nc.scalar.copy, x_op[0], x_rows, 3 * P, P)
        quantise(x_op, 0, 2 * P)
        quantise(x_op, 2 * P, 2 * P)

        adj_op = operand("adj")
        adj_words = adj_rows[:].bitcast(F32)
        adj_pairs = adj_op[0][:].bitcast(F32).rearrange("p (n u) -> p n u", u=2)
        for i in range(TILES):
            adjT = psum.tile([P, 2, P], F32, tag="bank")
            for u in range(2):
                first = (2 * i + u) * P
                nc.tensor.transpose(adjT[:, u, :], adj_words[:, first : first + P], ident[:])
            nc.scalar.copy(
                out=adj_pairs[:, i * P : (i + 1) * P, :], in_=adjT[:].rearrange("p u n -> p n u")
            )
        b_bank = psum.tile([P, SIZE], F32, tag="bank")
        nc.tensor.matmul(out=b_bank[:], lhsT=ones[:], rhs=b_rows[:], start=True, stop=True)
        b_all = keep.tile([P, SIZE], F32)
        nc.scalar.copy(out=b_all[:], in_=b_bank[:])

        quantise(adj_op, 0, P)
        quantise(adj_op, P, P)
        quantise(adj_op, 2 * P, 2 * P)

        w_op = operand("w")
        regroup(nc.vector.tensor_copy, w_op[0], w_rows, 0, 2 * P)
        regroup(nc.vector.tensor_copy, w_op[0], w_rows, 2 * P, 2 * P)
        quantise(w_op, 0, 2 * P)
        quantise(w_op, 2 * P, 2 * P)

        agg_op = operand("agg")
        agg_words = agg_op[0][:].rearrange("p (n t) -> p n t", t=PACK)
        for i in range(TILES):
            aggT = psum.tile([P, PACK, P], F32, tag="bank")
            for t in range(PACK):
                multiply(aggT[:, t, :], x_op, t * P, adj_op, i * P, P)
            nc.scalar.copy(
                out=agg_words[:, i * P : (i + 1) * P, :], in_=aggT[:].rearrange("p t n -> p n t")
            )
            if i != 1:
                first = P if i == 2 else i * P
                quantise(agg_op, first, (i + 1) * P - first)

        out_view = out[0].rearrange("(p i) k -> p i k", i=TILES)
        h_bank = {}
        h, g, sumsq, stats, eps_term, mean_var, inv_spread = {}, {}, {}, {}, {}, {}, {}

        def product(i):
            h_bank[i] = psum.tile([P, SIZE], F32, tag="bank", name="h_bank")
            multiply(h_bank[i][:], agg_op, i * P, w_op, 0, SIZE)

        def add_bias(i):
            h[i] = work.tile([P, SIZE], F32, name="h")
            nc.vector.tensor_tensor(out=h[i][:], in0=h_bank[i][:], in1=b_all[:], op=ALU.add)

        def relu(i):
            g[i] = work.tile([P, SIZE], F32, name="g")
            nc.scalar.activation(out=g[i][:], in_=h[i][:], func=ACT.Relu)

        def sum_of_squares(i):
            squares = work.tile([P, SIZE], F32)
            sumsq[i] = work.tile([P, 1], F32, name="sumsq")
            nc.scalar.activation(out=squares[:], in_=h[i][:], func=ACT.Square, accum_out=sumsq[i][:])

        def moments(i):
            stats[i] = work.tile([P, 6], F32, name="stats")
            nc.vector.bn_stats(out=stats[i][:], in_=g[i][:])

        def aggregate_moments(i):
            mean_var[i] = work.tile([P, 2], F32, name="mean_var")
            nc.vector.bn_aggr(out=mean_var[i][:], in_=stats[i][:])

        def epsilon_term(i):
            eps_term[i] = work.tile([P, 1], F32, name="eps_term")
            nc.vector.tensor_scalar(
                out=eps_term[i][:], in0=sumsq[i][:], scalar1=NORM_EPS * NORM_EPS, scalar2=BN_EPS,
                op0=ALU.max, op1=ALU.mult,
            )

        def inverse_root(i):
            inv_spread[i] = work.tile([P, 1], F32, name="inv_spread")
            nc.scalar.activation(
                out=inv_spread[i][:], in_=eps_term[i][:], func=ACT.Abs_reciprocal_sqrt,
                bias=mean_var[i][:, 1:2],
            )

        def store(i, result):
            nc.sync.dma_start(out=out_view[:, i, :], in_=result[:])

        def normalise(i):
            result = work.tile([P, SIZE], F32, name="result")
            nc.vector.tensor_scalar(
                out=result[:], in0=g[i][:], scalar1=mean_var[i][:, 0:1], scalar2=inv_spread[i][:],
                op0=ALU.subtract, op1=ALU.mult,
            )
            store(i, result)

        for i in range(TILES):
            product(i)
        add_bias(0)
        add_bias(1)
        add_bias(2)
        relu(0)
        sum_of_squares(0)
        relu(1)
        moments(0)
        add_bias(3)
        epsilon_term(0)
        aggregate_moments(0)
        sum_of_squares(1)
        inverse_root(0)
        moments(1)
        relu(2)
        normalise(0)
        epsilon_term(1)
        aggregate_moments(1)
        sum_of_squares(2)
        inverse_root(1)
        moments(2)
        relu(3)
        normalise(1)
        epsilon_term(2)
        aggregate_moments(2)
        sum_of_squares(3)
        inverse_root(2)
        moments(3)
        epsilon_term(3)
        aggregate_moments(3)
        inverse_root(3)
        normalise(2)
        normalise(3)
